import numpy as np
import ml_dtypes


def mxq(x, axis, fmt="e4m3"):
    dtype, down = {"e4m3": (ml_dtypes.float8_e4m3fn, 7), "e5m2": (ml_dtypes.float8_e5m2, 14)}[fmt]
    v = np.moveaxis(np.asarray(x, np.float32).astype(ml_dtypes.bfloat16).astype(np.float64), axis, -1)
    blocks = v.reshape(v.shape[:-1] + (-1, 32))
    amax = np.abs(blocks).max(-1, keepdims=True)
    byte = np.maximum(np.where(amax > 0, np.frexp(amax)[1] - 1 + 127, 0) - down, 1)
    scale = np.exp2(byte - 127.0)
    codes = (blocks / scale).astype(np.float32).astype(dtype).astype(np.float64)
    return np.moveaxis((codes * scale).reshape(v.shape), -1, axis)


WIDE = False


def mx_kscale(k):
    if not WIDE:
        return np.ones(k)
    levels = np.array([10, -10, 5, -5, 0])
    a = np.random.permutation(np.resize(levels, k // 512 * 4)).reshape(k // 512, 4)
    idx = np.arange(k)
    return np.exp2(a[idx // 512, idx % 128 // 32])


BF16 = ml_dtypes.bfloat16


def bf(x):
    return np.asarray(x, np.float32).astype(BF16)


def f64(x):
    return np.asarray(x).astype(np.float64)


E2M1 = np.array([0.0, 0.5, 1.0, 1.5, 2.0, 3.0, 4.0, 6.0, -0.0, -0.5, -1.0, -1.5, -2.0, -3.0, -4.0, -6.0])


def pack_weight(w, fmt):
    k, n = w.shape
    w = f64(bf(w)).reshape(k // 32, 32, n)
    amax = np.abs(w).max(1)
    if fmt == "e4m3":
        byte = np.frexp(amax)[1] - 1 + 127 - 7
    else:
        mant, ex = np.frexp(amax / 6.0)
        byte = np.where(mant > 0.5, ex, ex - 1) + 127
    byte = np.clip(np.where(amax > 0, byte, 1), 1, 254)
    scaled = (w * np.exp2(127.0 - byte)[:, None, :]).reshape(k, n).astype(np.float32)
    by_word = np.ascontiguousarray(scaled.reshape(k // 512, 128, 4, n).transpose(0, 1, 3, 2))
    if fmt == "e4m3":
        words = by_word.astype(ml_dtypes.float8_e4m3fn).view(np.uint8)
    else:
        c = by_word.astype(ml_dtypes.float4_e2m1fn).view(np.uint8) & 0xF
        words = c[..., 0::2] | (c[..., 1::2] << 4)
    return np.ascontiguousarray(words), np.ascontiguousarray(byte.astype(np.uint8).reshape(k // 512, 16, n))


def unpack_weight(words, scales, fmt):
    g, p, n, _ = words.shape
    if fmt == "e4m3":
        vals = np.ascontiguousarray(words).view(ml_dtypes.float8_e4m3fn).astype(np.float64)
    else:
        nib = np.empty((g, p, n, 4), np.uint8)
        nib[..., 0::2] = words & 0xF
        nib[..., 1::2] = words >> 4
        vals = E2M1[nib]
    vals = vals * np.repeat(np.exp2(scales.astype(np.float64) - 127.0), 8, axis=1)[..., None]
    return vals.transpose(0, 1, 3, 2).reshape(g * 512, n)


S, B, ND, NS, HN, BT, C, Hd, Wd = 8, 16, 32, 96, 4096, 2048, 3, 32, 64
P = C * Hd * Wd
EPS = 1e-9
SELU_ALPHA = 1.6732632423543772848170429916717
SELU_SCALE = 1.0507009873554804934193349852946


def selu(v):
    return SELU_SCALE * np.where(v > 0, v, SELU_ALPHA * np.expm1(np.minimum(v, 0.0)))


def sigmoid(v):
    return 1.0 / (1.0 + np.exp(-v))


def setup_inputs():
    t = mx_kscale(HN)
    digits = bf(np.random.random_sample((S, B, ND)))
    styles = bf(np.random.standard_normal((S, B, NS)))
    images = bf(np.random.random_sample((S, B, C, Hd, Wd)))
    W_h = bf(np.random.standard_normal((ND + NS, HN)) / np.sqrt(ND + NS) * t)
    b_h = bf(np.random.standard_normal(HN) * 0.5 * t)
    W1_words, W1_scales = pack_weight(np.random.standard_normal((HN, BT)) * 1.4 / np.sqrt(HN) / t[:, None], "e4m3")
    b1 = bf(np.random.standard_normal(BT) * 0.5)
    W2_words, W2_scales = pack_weight(np.random.standard_normal((BT, P)) / np.sqrt(BT), "e4m3")
    b2 = bf(np.random.standard_normal(P) * 0.5)
    return {"digits": digits,
            "styles": styles,
            "images": images,
            "W_h": W_h,
            "b_h": b_h,
            "W1_words": W1_words,
            "W1_scales": W1_scales,
            "b1": b1,
            "W2_words": W2_words,
            "W2_scales": W2_scales,
            "b2": b2}


def reference(digits, styles, images, W_h, b_h, W1_words, W1_scales, b1, W2_words, W2_scales, b2):
    h = np.maximum(np.concatenate([f64(digits), f64(styles)], axis=-1) @ f64(W_h) + f64(b_h), 0.0)
    t = selu((mxq(h, 2, "e4m3") @ unpack_weight(W1_words, W1_scales, "e4m3")) + f64(b1))
    x_hat = sigmoid((mxq(t, 2, "e4m3") @ unpack_weight(W2_words, W2_scales, "e4m3")) + f64(b2))
    images_mean = x_hat.reshape(x_hat.shape[0], x_hat.shape[1], C, Hd, Wd)
    img = f64(images)
    loss = -(np.log(images_mean + EPS) * img + np.log(1.0 - images_mean + EPS) * (1.0 - img)).sum(-1)
    return loss

@@ -1,0 +1,343 @@
+from contextlib import ExitStack
+
+import concourse.mybir as mybir
+from concourse.masks import make_identity
+
+FLOPS = 2 * 128 * (128 * 4096 + 4096 * 2048 + 2048 * 6144)
+
+F32 = mybir.dt.float32
+BF16 = mybir.dt.bfloat16
+I32 = mybir.dt.int32
+U32 = mybir.dt.uint32
+U8 = mybir.dt.uint8
+FP8X4 = mybir.dt.float8_e4m3fn_x4
+ACT = mybir.ActivationFunctionType
+ALU = mybir.AluOpType
+AX = mybir.AxisListType
+
+P = 128
+EPS = 1e-9
+SELU_ALPHA = 1.6732632423543772848170429916717
+SELU_SCALE = 1.0507009873554804934193349852946
+SA = SELU_SCALE * SELU_ALPHA
+
+PINNED = True
+GW = 2048
+NG = 3
+PIECE = 512
+SPLIT = 1
+
+
+def tile_decoder_w_kernel(
+    tc, digits, styles, images, W_h, b_h, W1_words, W1_scales, b1, W2_words, W2_scales, b2, out
+):
+    nc = tc.nc
+    with ExitStack() as ctx:
+        if PINNED:
+            ctx.enter_context(tc.manual_schedule())
+        const = ctx.enter_context(tc.tile_pool(name="const", bufs=1))
+        wpool = ctx.enter_context(tc.tile_pool(name="wpool", bufs=12))
+        work = ctx.enter_context(tc.tile_pool(name="work", bufs=2))
+        xpool = ctx.enter_context(tc.tile_pool(name="xpool", bufs=2))
+        accp = ctx.enter_context(tc.psum_pool(name="accp", bufs=4))
+        misc = ctx.enter_context(tc.psum_pool(name="misc", bufs=4))
+
+        w1pl = const.tile([P, 2, 2048], U8, name="w1pl", align_bytes=64)
+        w2pl = const.tile([P, 6144], U8, name="w2pl", align_bytes=64)
+        rows = const.tile([P, 512], BF16, name="rows")
+        eps_t = const.tile([P, 1], F32, name="eps_t")
+        warm = const.tile([P, 1], F32, name="warm")
+        nc.vector.memset(rows[:], 0.0)
+        nc.vector.memset(w1pl[:].bitcast(I32), 0)
+        nc.vector.memset(w2pl[:].bitcast(I32), 0)
+        nc.vector.memset(eps_t[:], EPS)
+        ident = const.tile([P, P], BF16, name="ident")
+        make_identity(nc, ident[:])
+
+        cat_sb = const.tile([P, P], BF16, name="cat_sb")
+        catT = const.tile([P, P], BF16, name="catT")
+        wh = const.tile([P, 4096], BF16, name="wh")
+        bhT = const.tile([P, 4, 8], F32, name="bhT")
+        b1b = const.tile([P, 2048], BF16, name="b1b")
+        b2b = const.tile([P, 6144], BF16, name="b2b")
+        img = const.tile([P, 6144], BF16, name="img")
+        hcodes = const.tile([P, 8, P], U32, name="hcodes", align_bytes=64)
+        hplanes = const.tile([P, 8, P], U8, name="hplanes", align_bytes=64)
+        tcodes = const.tile([P, 4, P], U32, name="tcodes", align_bytes=64)
+        tplanes = const.tile([P, 4, P], U8, name="tplanes", align_bytes=64)
+        loss = const.tile([P, 96], F32, name="loss")
+
+        nc.scalar.dma_start(out=rows[16:24, :], in_=b_h.rearrange("(r n) -> r n", n=512))
+        nc.scalar.dma_start(out=rows[12:16, :], in_=b1.rearrange("(r n) -> r n", n=512))
+        nc.scalar.dma_start(out=rows[0:12, :], in_=b2.rearrange("(r n) -> r n", n=512))
+        nc.scalar.dma_start(out=cat_sb[:, 0:32], in_=digits.rearrange("s b d -> (s b) d"))
+        nc.scalar.dma_start(out=cat_sb[:, 32:128], in_=styles.rearrange("s b d -> (s b) d"))
+        nc.scalar.activation(out=warm[:], in_=eps_t[:], func=ACT.Exp)
+        for hf in range(2):
+            for q in range(4):
+                nc.sync.dma_start(
+                    out=w1pl[32 * q : 32 * q + 16, hf, :].bitcast(I32),
+                    in_=W1_scales[4 * hf : 4 * hf + 4, 4 * q : 4 * q + 4, :].bitcast(I32),
+                )
+        for q in range(4):
+            nc.sync.dma_start(
+                out=w2pl[32 * q : 32 * q + 16, :].bitcast(I32),
+                in_=W2_scales[:, 4 * q : 4 * q + 4, :].bitcast(I32),
+            )
+        nc.sync.dma_start(out=wh[:], in_=W_h)
+
+        wt = {}
+        img_v = images.rearrange("s b c h w -> (s b) (c h w)")
+
+        def load_next(i):
+            if i < 6:
+                t_ = wpool.tile([P, 2048], U32, name="w1_%d" % i, tag="w", align_bytes=64)
+                nc.sync.dma_start(
+                    out=t_[:].bitcast(I32),
+                    in_=W1_words[i].rearrange("p n t -> p (n t)").bitcast(I32),
+                )
+            elif i < 10:
+                b = i - 6
+                t_ = wpool.tile([P, 2, 512], U32, name="w1e_%d" % b, tag="w", align_bytes=64)
+                nc.sync.dma_start(
+                    out=t_[:].bitcast(I32),
+                    in_=W1_words[6:8, :, 512 * b : 512 * (b + 1), :]
+                    .rearrange("g p n t -> p g (n t)")
+                    .bitcast(I32),
+                )
+            else:
+                k = i - 10
+                q = k // 4
+                g = k % 4
+                t_ = wpool.tile([P, GW], U32, name="w2_%d" % k, tag="w", align_bytes=64)
+                nc.sync.dma_start(
+                    out=t_[:].bitcast(I32),
+                    in_=W2_words[g, :, GW * q : GW * (q + 1), :].rearrange("p n t -> p (n t)").bitcast(I32),
+                )
+                if g == 3:
+                    nc.sync.dma_start(out=img[:, GW * q : GW * (q + 1)], in_=img_v[:, GW * q : GW * (q + 1)])
+            wt[i] = t_
+
+        for i in range(12):
+            load_next(i)
+
+        psb = misc.tile([P, 4, P], BF16, name="psb", tag="misc")
+        for t in range(4):
+            nc.tensor.transpose(out=psb[:, t, :], in_=rows[:, t:512:4], identity=ident[:])
+        nc.vector.tensor_copy(out=bhT[:], in_=psb[:, :, 16:24])
+
+        for r in range(16):
+            pb = misc.tile([P, 512], F32, name="pb", tag="misc")
+            nc.tensor.matmul(
+                out=pb[:],
+                lhsT=ident[:, r : r + 1].to_broadcast([P, P]),
+                rhs=rows[:],
+                start=True,
+                stop=True,
+            )
+            if r < 12:
+                dst = b2b[:, 512 * r : 512 * (r + 1)]
+            else:
+                dst = b1b[:, 512 * (r - 12) : 512 * (r - 11)]
+            if r % 2 == 0:
+                nc.vector.tensor_copy(out=dst, in_=pb[:])
+            else:
+                nc.scalar.copy(out=dst, in_=pb[:])
+
+        psc = misc.tile([P, P], BF16, name="psc", tag="misc")
+        nc.tensor.transpose(out=psc[:], in_=cat_sb[:], identity=ident[:])
+        nc.vector.tensor_copy(out=catT[:], in_=psc[:])
+
+        def layer0(g):
+            ps0 = misc.tile([P, 4, P], F32, name="ps0", tag="misc")
+            hb = work.tile([P, 4, P], BF16, name="hb")
+            for t in range(4):
+                nc.tensor.matmul(
+                    out=ps0[:, t, :],
+                    lhsT=wh[:, 512 * g + t : 512 * (g + 1) : 4],
+                    rhs=catT[:],
+                    start=True,
+                    stop=True,
+                )
+            for t in range(4):
+                nc.scalar.activation(
+                    out=hb[:, t, :], in_=ps0[:, t, :], func=ACT.Relu, bias=bhT[:, t, g : g + 1]
+                )
+            hg = work.tile([P, P, 4], BF16, name="hg", align_bytes=64)
+            nc.vector.tensor_copy(out=hg[:], in_=hb[:].rearrange("p t w -> p w t"))
+            nc.vector.quantize_mx(
+                out=hcodes[:, g, :].bitcast(FP8X4),
+                scales=hplanes[:, g, :],
+                in_=hg[:].rearrange("p w t -> p (w t)"),
+            )
+
+        acc = []
+        for b in range(4):
+            acc_t = accp.tile([P, 512], F32, name="acc%d" % b, tag="acc")
+            acc.append(acc_t)
+
+        def l1_pass(g, b, rhs):
+            nc.tensor.matmul_mx(
+                out=acc[b][:],
+                lhsT=hcodes[:, g, :].bitcast(FP8X4),
+                lhsT_scale=hplanes[:, g, :],
+                rhs=rhs.bitcast(FP8X4),
+                rhs_scale=w1pl[4 * (g % 4) : P, g // 4, 512 * b : 512 * (b + 1)],
+                start=(g == 0),
+                stop=(g == 7),
+            )
+
+        layer0(0)
+        layer0(1)
+        for g in range(6):
+            layer0(g + 2)
+            for b in range(4):
+                l1_pass(g, b, wt[g][:, 512 * b : 512 * (b + 1)])
+            load_next(12 + g)
+
+        x2s = {}
+        pss = {}
+
+        def l2_pass(q, g):
+            for b in range(4):
+                if g == 0:
+                    if q % 2 == 0:
+                        ps_t = accp.tile([P, 512], F32, name="ps_a", tag="acc")
+                    else:
+                        ps_t = misc.tile([P, 512], F32, name="ps_m", tag="misc")
+                    pss[(q, b)] = ps_t
+                col = GW * q + 512 * b
+                nc.tensor.matmul_mx(
+                    out=pss[(q, b)][:],
+                    lhsT=tcodes[:, g, :].bitcast(FP8X4),
+                    lhsT_scale=tplanes[:, g, :],
+                    rhs=wt[10 + 4 * q + g][:, 512 * b : 512 * (b + 1)].bitcast(FP8X4),
+                    rhs_scale=w2pl[4 * g : P, col : col + 512],
+                    start=(g == 0),
+                    stop=(g == 3),
+                )
+
+        def add_bias(q):
+            x2 = xpool.tile([P, 2, GW], F32, name="x2", tag="x2")
+            x2s[q] = x2
+            for b in range(4):
+                col = GW * q + 512 * b
+                nc.vector.tensor_tensor(
+                    out=x2[:, 0, 512 * b : 512 * (b + 1)],
+                    in0=pss[(q, b)][:],
+                    in1=b2b[:, col : col + 512],
+                    op=ALU.add,
+                )
+
+        def sigmoids(q):
+            x2 = x2s[q]
+            for lo in range(0, GW, 1024):
+                nc.scalar.activation(
+                    out=x2[:, 0, lo : lo + 1024], in_=x2[:, 0, lo : lo + 1024], func=ACT.Sigmoid
+                )
+                nc.gpsimd.tensor_scalar(
+                    out=x2[:, 1, lo : lo + 1024],
+                    in0=x2[:, 0, lo : lo + 1024],
+                    scalar1=-1.0,
+                    scalar2=1.0,
+                    op0=ALU.mult,
+                    op1=ALU.add,
+                )
+
+        def logs(q):
+            x2 = x2s[q]
+            for lo in range(0, GW, PIECE):
+                nc.scalar.activation(
+                    out=x2[:, :, lo : lo + PIECE], in_=x2[:, :, lo : lo + PIECE], func=ACT.Ln, bias=eps_t[:]
+                )
+
+        def weigh_and_sum(q, lo):
+            x2 = x2s[q]
+            nc.gpsimd.tensor_tensor(
+                out=x2[:, 0, lo : lo + PIECE],
+                in0=x2[:, 0, lo : lo + PIECE],
+                in1=x2[:, 1, lo : lo + PIECE],
+                op=ALU.subtract,
+            )
+            nc.vector.tensor_tensor(
+                out=x2[:, 0, lo : lo + PIECE],
+                in0=x2[:, 0, lo : lo + PIECE],
+                in1=img[:, GW * q + lo : GW * q + lo + PIECE],
+                op=ALU.mult,
+            )
+            j0 = (GW * q + lo) // 64
+            nc.vector.tensor_reduce(
+                out=loss[:, j0 : j0 + PIECE // 64],
+                in_=x2[:, :, lo : lo + PIECE].rearrange("p a (j w) -> p j a w", w=64),
+                axis=AX.XY,
+                op=ALU.add,
+                negate=True,
+            )
+
+        vs = {}
+        es = {}
+        rs = {}
+        tgs = {}
+
+        def stage_a(b):
+            for g in range(6, 8):
+                l1_pass(g, b, wt[6 + b][:, g - 6, :])
+            load_next(18 + b)
+            v = work.tile([P, 512], F32, name="v", bufs=3)
+            e = work.tile([P, 512], F32, name="e", bufs=3)
+            a = work.tile([P, 512], F32, name="a", bufs=3)
+            nc.vector.tensor_tensor(out=v[:], in0=acc[b][:], in1=b1b[:, 512 * b : 512 * (b + 1)], op=ALU.add)
+            nc.scalar.activation(out=e[:], in_=v[:], func=ACT.Exp)
+            nc.scalar.activation(out=a[:], in_=v[:], func=ACT.Relu, scale=SELU_SCALE)
+            vs[b] = v
+            es[b] = e
+            rs[b] = a
+
+        def stage_b(b):
+            tb = work.tile([P, 512], BF16, name="tb")
+            nc.vector.tensor_scalar(
+                out=es[b][:], in0=es[b][:], scalar1=1.0, scalar2=SA, op0=ALU.min, op1=ALU.mult
+            )
+            nc.vector.scalar_tensor_tensor(
+                out=tb[:], in0=es[b][:], scalar=-SA, in1=rs[b][:], op0=ALU.add, op1=ALU.add
+            )
+            pst = misc.tile([P, 4, P], BF16, name="pst", tag="misc")
+            for t in range(4):
+                nc.tensor.transpose(out=pst[:, t, :], in_=tb[:, t:512:4], identity=ident[:])
+            tg = work.tile([P, P, 4], BF16, name="tg", align_bytes=64)
+            nc.scalar.copy(out=tg[:], in_=pst[:].rearrange("p t w -> p w t"))
+            tgs[b] = tg
+
+        def stage_c(b):
+            nc.vector.quantize_mx(
+                out=tcodes[:, b, :].bitcast(FP8X4),
+                scales=tplanes[:, b, :],
+                in_=tgs[b][:].rearrange("p w t -> p (w t)"),
+            )
+
+        for i in range(7):
+            if i < 4:
+                stage_a(i)
+            if 1 <= i < 5:
+                stage_b(i - 1)
+            if 2 <= i < 6:
+                stage_c(i - 2)
+            if i >= 3:
+                l2_pass(0, i - 3)
+
+        out_v = out.rearrange("s b c h -> (s b) (c h)")
+        add_bias(0)
+        sigmoids(0)
+        for q in range(NG):
+            logs(q)
+            if q + 1 < NG:
+                for g in range(4):
+                    l2_pass(q + 1, g)
+            for i in range(GW // PIECE):
+                if i == SPLIT and q + 1 < NG:
+                    add_bias(q + 1)
+                weigh_and_sum(q, PIECE * i)
+            if q + 1 < NG:
+                sigmoids(q + 1)
+            j0 = GW * q // 64
+            nc.sync.dma_start(out=out_v[:, j0 : j0 + GW // 64], in_=loss[:, j0 : j0 + GW // 64])

@@ -26,6 +26,8 @@ GW = 2048
 NG = 3
 PIECE = 512
 SPLIT = 1
+Y_ON_VECTOR = True
+D_ON_VECTOR = True
 
 
 def tile_decoder_w_kernel(
@@ -235,7 +237,12 @@ def tile_decoder_w_kernel(
                 nc.scalar.activation(
                     out=x2[:, 0, lo : lo + 1024], in_=x2[:, 0, lo : lo + 1024], func=ACT.Sigmoid
                 )
-                nc.gpsimd.tensor_scalar(
+
+        def complements(q):
+            x2 = x2s[q]
+            eng = nc.vector if Y_ON_VECTOR else nc.gpsimd
+            for lo in range(0, GW, 1024):
+                eng.tensor_scalar(
                     out=x2[:, 1, lo : lo + 1024],
                     in0=x2[:, 0, lo : lo + 1024],
                     scalar1=-1.0,
@@ -253,7 +260,8 @@ def tile_decoder_w_kernel(
 
         def weigh_and_sum(q, lo):
             x2 = x2s[q]
-            nc.gpsimd.tensor_tensor(
+            eng = nc.vector if D_ON_VECTOR else nc.gpsimd
+            eng.tensor_tensor(
                 out=x2[:, 0, lo : lo + PIECE],
                 in0=x2[:, 0, lo : lo + PIECE],
                 in1=x2[:, 1, lo : lo + PIECE],
@@ -328,6 +336,7 @@ def tile_decoder_w_kernel(
         out_v = out.rearrange("s b c h -> (s b) (c h)")
         add_bias(0)
         sigmoids(0)
+        complements(0)
         for q in range(NG):
             logs(q)
             if q + 1 < NG:
@@ -336,8 +345,9 @@ def tile_decoder_w_kernel(
             for i in range(GW // PIECE):
                 if i == SPLIT and q + 1 < NG:
                     add_bias(q + 1)
+                    sigmoids(q + 1)
+                if i == SPLIT + 1 and q + 1 < NG:
+                    complements(q + 1)
                 weigh_and_sum(q, PIECE * i)
-            if q + 1 < NG:
-                sigmoids(q + 1)
             j0 = GW * q // 64
             nc.sync.dma_start(out=out_v[:, j0 : j0 + GW // 64], in_=loss[:, j0 : j0 + GW // 64])

@@ -26,8 +26,7 @@ GW = 2048
 NG = 3
 PIECE = 512
 SPLIT = 1
-Y_ON_VECTOR = True
-D_ON_VECTOR = True
+Y_ON_VECTOR = False
 
 
 def tile_decoder_w_kernel(
@@ -258,21 +257,30 @@ def tile_decoder_w_kernel(
                     out=x2[:, :, lo : lo + PIECE], in_=x2[:, :, lo : lo + PIECE], func=ACT.Ln, bias=eps_t[:]
                 )
 
-        def weigh_and_sum(q, lo):
+        def difference(q, i):
             x2 = x2s[q]
-            eng = nc.vector if D_ON_VECTOR else nc.gpsimd
+            lo = PIECE * i
+            eng = nc.vector if i % 2 == 0 else nc.gpsimd
             eng.tensor_tensor(
                 out=x2[:, 0, lo : lo + PIECE],
                 in0=x2[:, 0, lo : lo + PIECE],
                 in1=x2[:, 1, lo : lo + PIECE],
                 op=ALU.subtract,
             )
+
+        def weigh(q, i):
+            x2 = x2s[q]
+            lo = PIECE * i
             nc.vector.tensor_tensor(
                 out=x2[:, 0, lo : lo + PIECE],
                 in0=x2[:, 0, lo : lo + PIECE],
                 in1=img[:, GW * q + lo : GW * q + lo + PIECE],
                 op=ALU.mult,
             )
+
+        def total(q, i):
+            x2 = x2s[q]
+            lo = PIECE * i
             j0 = (GW * q + lo) // 64
             nc.vector.tensor_reduce(
                 out=loss[:, j0 : j0 + PIECE // 64],
@@ -342,12 +350,18 @@ def tile_decoder_w_kernel(
             if q + 1 < NG:
                 for g in range(4):
                     l2_pass(q + 1, g)
-            for i in range(GW // PIECE):
-                if i == SPLIT and q + 1 < NG:
+            n_pieces = GW // PIECE
+            for k in range(n_pieces + 2):
+                if k == SPLIT and q + 1 < NG:
                     add_bias(q + 1)
                     sigmoids(q + 1)
-                if i == SPLIT + 1 and q + 1 < NG:
-                    complements(q + 1)
-                weigh_and_sum(q, PIECE * i)
+                if k < n_pieces:
+                    difference(q, k)
+                if 1 <= k <= n_pieces:
+                    weigh(q, k - 1)
+                if k >= 2:
+                    total(q, k - 2)
+            if q + 1 < NG:
+                complements(q + 1)
             j0 = GW * q // 64
             nc.sync.dma_start(out=out_v[:, j0 : j0 + GW // 64], in_=loss[:, j0 : j0 + GW // 64])

@@ -46,10 +46,12 @@ def tile_decoder_w_kernel(
         w1pl = const.tile([P, 2, 2048], U8, name="w1pl", align_bytes=64)
         w2pl = const.tile([P, 6144], U8, name="w2pl", align_bytes=64)
         rows = const.tile([P, 512], BF16, name="rows")
+        rows_h = const.tile([P, 512], BF16, name="rows_h")
         eps_t = const.tile([P, 1], F32, name="eps_t")
         warm = const.tile([P, 1], F32, name="warm")
-        nc.vector.memset(rows[:], 0.0)
+        nc.vector.memset(rows_h[:], 0.0)
         nc.vector.memset(w1pl[:].bitcast(I32), 0)
+        nc.vector.memset(rows[:], 0.0)
         nc.vector.memset(w2pl[:].bitcast(I32), 0)
         nc.vector.memset(eps_t[:], EPS)
         ident = const.tile([P, P], BF16, name="ident")
@@ -68,24 +70,28 @@ def tile_decoder_w_kernel(
         tplanes = const.tile([P, 4, P], U8, name="tplanes", align_bytes=64)
         loss = const.tile([P, 96], F32, name="loss")
 
-        nc.scalar.dma_start(out=rows[16:24, :], in_=b_h.rearrange("(r n) -> r n", n=512))
-        nc.scalar.dma_start(out=rows[12:16, :], in_=b1.rearrange("(r n) -> r n", n=512))
-        nc.scalar.dma_start(out=rows[0:12, :], in_=b2.rearrange("(r n) -> r n", n=512))
+        nc.scalar.dma_start(out=rows_h[0:8, :], in_=b_h.rearrange("(r n) -> r n", n=512))
         nc.scalar.dma_start(out=cat_sb[:, 0:32], in_=digits.rearrange("s b d -> (s b) d"))
         nc.scalar.dma_start(out=cat_sb[:, 32:128], in_=styles.rearrange("s b d -> (s b) d"))
         nc.scalar.activation(out=warm[:], in_=eps_t[:], func=ACT.Exp)
-        for hf in range(2):
-            for q in range(4):
-                nc.sync.dma_start(
-                    out=w1pl[32 * q : 32 * q + 16, hf, :].bitcast(I32),
-                    in_=W1_scales[4 * hf : 4 * hf + 4, 4 * q : 4 * q + 4, :].bitcast(I32),
-                )
+        nc.sync.dma_start(out=wh[:], in_=W_h)
         for q in range(4):
             nc.sync.dma_start(
-                out=w2pl[32 * q : 32 * q + 16, :].bitcast(I32),
-                in_=W2_scales[:, 4 * q : 4 * q + 4, :].bitcast(I32),
+                out=w1pl[32 * q : 32 * q + 16, 0, :].bitcast(I32),
+                in_=W1_scales[0:4, 4 * q : 4 * q + 4, :].bitcast(I32),
             )
-        nc.sync.dma_start(out=wh[:], in_=W_h)
+        nc.gpsimd.dma_start(out=rows[12:16, :], in_=b1.rearrange("(r n) -> r n", n=512))
+        nc.gpsimd.dma_start(out=rows[0:12, :], in_=b2.rearrange("(r n) -> r n", n=512))
+        for q in range(4):
+            nc.gpsimd.dma_start(
+                out=w1pl[32 * q : 32 * q + 16, 1, :].bitcast(F32),
+                in_=W1_scales[4:8, 4 * q : 4 * q + 4, :].bitcast(F32),
+            )
+        for q in range(4):
+            nc.gpsimd.dma_start(
+                out=w2pl[32 * q : 32 * q + 16, :].bitcast(F32),
+                in_=W2_scales[:, 4 * q : 4 * q + 4, :].bitcast(F32),
+            )
 
         wt = {}
         img_v = images.rearrange("s b c h w -> (s b) (c h w)")
@@ -124,10 +130,13 @@ def tile_decoder_w_kernel(
 
         psb = misc.tile([P, 4, P], BF16, name="psb", tag="misc")
         for t in range(4):
-            nc.tensor.transpose(out=psb[:, t, :], in_=rows[:, t:512:4], identity=ident[:])
-        nc.vector.tensor_copy(out=bhT[:], in_=psb[:, :, 16:24])
+            nc.tensor.transpose(out=psb[:, t, :], in_=rows_h[:, t:512:4], identity=ident[:])
+        nc.vector.tensor_copy(out=bhT[:], in_=psb[:, :, 0:8])
+        psc = misc.tile([P, P], BF16, name="psc", tag="misc")
+        nc.tensor.transpose(out=psc[:], in_=cat_sb[:], identity=ident[:])
+        nc.vector.tensor_copy(out=catT[:], in_=psc[:])
 
-        for r in range(16):
+        def spread(r):
             pb = misc.tile([P, 512], F32, name="pb", tag="misc")
             nc.tensor.matmul(
                 out=pb[:],
@@ -144,10 +153,6 @@ def tile_decoder_w_kernel(
                 nc.vector.tensor_copy(out=dst, in_=pb[:])
             else:
                 nc.scalar.copy(out=dst, in_=pb[:])
-
-        psc = misc.tile([P, P], BF16, name="psc", tag="misc")
-        nc.tensor.transpose(out=psc[:], in_=cat_sb[:], identity=ident[:])
-        nc.vector.tensor_copy(out=catT[:], in_=psc[:])
 
         def layer0(g):
             ps0 = misc.tile([P, 4, P], F32, name="ps0", tag="misc")
@@ -188,10 +193,13 @@ def tile_decoder_w_kernel(
                 stop=(g == 7),
             )
 
+        spread_order = [12, 13, 14, 15] + list(range(12))
         layer0(0)
         layer0(1)
         for g in range(6):
             layer0(g + 2)
+            for r in spread_order[(16 * g + 5) // 6 : (16 * (g + 1) + 5) // 6]:
+                spread(r)
             for b in range(4):
                 l1_pass(g, b, wt[g][:, 512 * b : 512 * (b + 1)])
             load_next(12 + g)

@@ -50,8 +50,8 @@ def tile_decoder_w_kernel(
         eps_t = const.tile([P, 1], F32, name="eps_t")
         warm = const.tile([P, 1], F32, name="warm")
         nc.vector.memset(rows_h[:], 0.0)
-        nc.vector.memset(w1pl[:].bitcast(I32), 0)
         nc.vector.memset(rows[:], 0.0)
+        nc.vector.memset(w1pl[:].bitcast(I32), 0)
         nc.vector.memset(w2pl[:].bitcast(I32), 0)
         nc.vector.memset(eps_t[:], EPS)
         ident = const.tile([P, P], BF16, name="ident")
@@ -73,6 +73,8 @@ def tile_decoder_w_kernel(
         nc.scalar.dma_start(out=rows_h[0:8, :], in_=b_h.rearrange("(r n) -> r n", n=512))
         nc.scalar.dma_start(out=cat_sb[:, 0:32], in_=digits.rearrange("s b d -> (s b) d"))
         nc.scalar.dma_start(out=cat_sb[:, 32:128], in_=styles.rearrange("s b d -> (s b) d"))
+        nc.scalar.dma_start(out=rows[12:16, :], in_=b1.rearrange("(r n) -> r n", n=512))
+        nc.scalar.dma_start(out=rows[0:12, :], in_=b2.rearrange("(r n) -> r n", n=512))
         nc.scalar.activation(out=warm[:], in_=eps_t[:], func=ACT.Exp)
         nc.sync.dma_start(out=wh[:], in_=W_h)
         for q in range(4):
@@ -80,8 +82,6 @@ def tile_decoder_w_kernel(
                 out=w1pl[32 * q : 32 * q + 16, 0, :].bitcast(I32),
                 in_=W1_scales[0:4, 4 * q : 4 * q + 4, :].bitcast(I32),
             )
-        nc.gpsimd.dma_start(out=rows[12:16, :], in_=b1.rearrange("(r n) -> r n", n=512))
-        nc.gpsimd.dma_start(out=rows[0:12, :], in_=b2.rearrange("(r n) -> r n", n=512))
         for q in range(4):
             nc.gpsimd.dma_start(
                 out=w1pl[32 * q : 32 * q + 16, 1, :].bitcast(F32),
@@ -198,11 +198,11 @@ def tile_decoder_w_kernel(
         layer0(1)
         for g in range(6):
             layer0(g + 2)
-            for r in spread_order[(16 * g + 5) // 6 : (16 * (g + 1) + 5) // 6]:
-                spread(r)
             for b in range(4):
                 l1_pass(g, b, wt[g][:, 512 * b : 512 * (b + 1)])
             load_next(12 + g)
+            for r in spread_order[(16 * g + 5) // 6 : (16 * (g + 1) + 5) // 6]:
+                spread(r)
 
         x2s = {}
         pss = {}
@@ -240,9 +240,9 @@ def tile_decoder_w_kernel(
 
         def sigmoids(q):
             x2 = x2s[q]
-            for lo in range(0, GW, 1024):
+            for lo in range(0, GW, 512):
                 nc.scalar.activation(
-                    out=x2[:, 0, lo : lo + 1024], in_=x2[:, 0, lo : lo + 1024], func=ACT.Sigmoid
+                    out=x2[:, 0, lo : lo + 512], in_=x2[:, 0, lo : lo + 512], func=ACT.Sigmoid
                 )
 
         def complements(q):
@@ -312,7 +312,9 @@ def tile_decoder_w_kernel(
             a = work.tile([P, 512], F32, name="a", bufs=3)
             nc.vector.tensor_tensor(out=v[:], in0=acc[b][:], in1=b1b[:, 512 * b : 512 * (b + 1)], op=ALU.add)
             nc.scalar.activation(out=e[:], in_=v[:], func=ACT.Exp)
-            nc.scalar.activation(out=a[:], in_=v[:], func=ACT.Relu, scale=SELU_SCALE)
+            nc.vector.tensor_scalar(
+                out=a[:], in0=v[:], scalar1=0.0, scalar2=SELU_SCALE, op0=ALU.max, op1=ALU.mult
+            )
             vs[b] = v
             es[b] = e
             rs[b] = a

@@ -25,7 +25,7 @@ PINNED = True
 GW = 2048
 NG = 3
 PIECE = 512
-SPLIT = 1
+SPLIT = 2
 Y_ON_VECTOR = False
 
 
@@ -198,11 +198,11 @@ def tile_decoder_w_kernel(
         layer0(1)
         for g in range(6):
             layer0(g + 2)
+            for r in spread_order[4 * g : 4 * g + 4]:
+                spread(r)
             for b in range(4):
                 l1_pass(g, b, wt[g][:, 512 * b : 512 * (b + 1)])
             load_next(12 + g)
-            for r in spread_order[(16 * g + 5) // 6 : (16 * (g + 1) + 5) // 6]:
-                spread(r)
 
         x2s = {}
         pss = {}
@@ -303,18 +303,18 @@ def tile_decoder_w_kernel(
         rs = {}
         tgs = {}
 
-        def stage_a(b):
+        for b in range(4):
             for g in range(6, 8):
                 l1_pass(g, b, wt[6 + b][:, g - 6, :])
             load_next(18 + b)
+
+        def stage_a(b):
             v = work.tile([P, 512], F32, name="v", bufs=3)
             e = work.tile([P, 512], F32, name="e", bufs=3)
             a = work.tile([P, 512], F32, name="a", bufs=3)
             nc.vector.tensor_tensor(out=v[:], in0=acc[b][:], in1=b1b[:, 512 * b : 512 * (b + 1)], op=ALU.add)
             nc.scalar.activation(out=e[:], in_=v[:], func=ACT.Exp)
-            nc.vector.tensor_scalar(
-                out=a[:], in0=v[:], scalar1=0.0, scalar2=SELU_SCALE, op0=ALU.max, op1=ALU.mult
-            )
+            nc.scalar.activation(out=a[:], in_=v[:], func=ACT.Relu, scale=SELU_SCALE)
             vs[b] = v
             es[b] = e
             rs[b] = a

@@ -69,6 +69,8 @@ def tile_decoder_w_kernel(
         tcodes = const.tile([P, 4, P], U32, name="tcodes", align_bytes=64)
         tplanes = const.tile([P, 4, P], U8, name="tplanes", align_bytes=64)
         loss = const.tile([P, 96], F32, name="loss")
+        sum_l2 = const.tile([P, GW // 64], F32, name="sum_l2")
+        sum_e = const.tile([P, GW // 64], F32, name="sum_e")
 
         nc.scalar.dma_start(out=rows_h[0:8, :], in_=b_h.rearrange("(r n) -> r n", n=512))
         nc.scalar.dma_start(out=cat_sb[:, 0:32], in_=digits.rearrange("s b d -> (s b) d"))
@@ -261,15 +263,27 @@ def tile_decoder_w_kernel(
         def logs(q):
             x2 = x2s[q]
             for lo in range(0, GW, PIECE):
-                nc.scalar.activation(
-                    out=x2[:, :, lo : lo + PIECE], in_=x2[:, :, lo : lo + PIECE], func=ACT.Ln, bias=eps_t[:]
-                )
+                if q + 1 < NG:
+                    nc.scalar.activation(
+                        out=x2[:, :, lo : lo + PIECE], in_=x2[:, :, lo : lo + PIECE], func=ACT.Ln, bias=eps_t[:]
+                    )
+                else:
+                    nc.scalar.activation(
+                        out=x2[:, 0, lo : lo + PIECE], in_=x2[:, 0, lo : lo + PIECE], func=ACT.Ln, bias=eps_t[:]
+                    )
+                    for c in range(lo, lo + PIECE, 64):
+                        nc.scalar.activation(
+                            out=x2[:, 1, c : c + 64],
+                            in_=x2[:, 1, c : c + 64],
+                            func=ACT.Ln,
+                            bias=eps_t[:],
+                            accum_out=sum_l2[:, c // 64 : c // 64 + 1],
+                        )
 
         def difference(q, i):
             x2 = x2s[q]
             lo = PIECE * i
-            eng = nc.vector if i % 2 == 0 else nc.gpsimd
-            eng.tensor_tensor(
+            nc.gpsimd.tensor_tensor(
                 out=x2[:, 0, lo : lo + PIECE],
                 in0=x2[:, 0, lo : lo + PIECE],
                 in1=x2[:, 1, lo : lo + PIECE],
@@ -290,13 +304,22 @@ def tile_decoder_w_kernel(
             x2 = x2s[q]
             lo = PIECE * i
             j0 = (GW * q + lo) // 64
-            nc.vector.tensor_reduce(
-                out=loss[:, j0 : j0 + PIECE // 64],
-                in_=x2[:, :, lo : lo + PIECE].rearrange("p a (j w) -> p j a w", w=64),
-                axis=AX.XY,
-                op=ALU.add,
-                negate=True,
-            )
+            if q + 1 < NG:
+                nc.vector.tensor_reduce(
+                    out=loss[:, j0 : j0 + PIECE // 64],
+                    in_=x2[:, :, lo : lo + PIECE].rearrange("p a (j w) -> p j a w", w=64),
+                    axis=AX.XY,
+                    op=ALU.add,
+                    negate=True,
+                )
+            else:
+                nc.vector.tensor_reduce(
+                    out=sum_e[:, lo // 64 : (lo + PIECE) // 64],
+                    in_=x2[:, 0, lo : lo + PIECE].rearrange("p (j w) -> p j w", w=64),
+                    axis=AX.X,
+                    op=ALU.add,
+                    negate=True,
+                )
 
         vs = {}
         es = {}
@@ -319,11 +342,13 @@ def tile_decoder_w_kernel(
             es[b] = e
             rs[b] = a
 
-        def stage_b(b):
-            tb = work.tile([P, 512], BF16, name="tb")
+        def stage_b0(b):
             nc.vector.tensor_scalar(
                 out=es[b][:], in0=es[b][:], scalar1=1.0, scalar2=SA, op0=ALU.min, op1=ALU.mult
             )
+
+        def stage_b(b):
+            tb = work.tile([P, 512], BF16, name="tb")
             nc.vector.scalar_tensor_tensor(
                 out=tb[:], in0=es[b][:], scalar=-SA, in1=rs[b][:], op0=ALU.add, op1=ALU.add
             )
@@ -345,9 +370,11 @@ def tile_decoder_w_kernel(
             if i < 4:
                 stage_a(i)
             if 1 <= i < 5:
-                stage_b(i - 1)
+                stage_b0(i - 1)
             if 2 <= i < 6:
                 stage_c(i - 2)
+            if 1 <= i < 5:
+                stage_b(i - 1)
             if i >= 3:
                 l2_pass(0, i - 3)
 
@@ -374,4 +401,6 @@ def tile_decoder_w_kernel(
             if q + 1 < NG:
                 complements(q + 1)
             j0 = GW * q // 64
+            if q + 1 == NG:
+                nc.vector.tensor_tensor(out=loss[:, j0 : j0 + GW // 64], in0=sum_e[:], in1=sum_l2[:], op=ALU.subtract)
             nc.sync.dma_start(out=out_v[:, j0 : j0 + GW // 64], in_=loss[:, j0 : j0 + GW // 64])

@@ -25,7 +25,7 @@ PINNED = True
 GW = 2048
 NG = 3
 PIECE = 512
-SPLIT = 2
+SPLIT = 3
 Y_ON_VECTOR = False
 
 
@@ -69,8 +69,6 @@ def tile_decoder_w_kernel(
         tcodes = const.tile([P, 4, P], U32, name="tcodes", align_bytes=64)
         tplanes = const.tile([P, 4, P], U8, name="tplanes", align_bytes=64)
         loss = const.tile([P, 96], F32, name="loss")
-        sum_l2 = const.tile([P, GW // 64], F32, name="sum_l2")
-        sum_e = const.tile([P, GW // 64], F32, name="sum_e")
 
         nc.scalar.dma_start(out=rows_h[0:8, :], in_=b_h.rearrange("(r n) -> r n", n=512))
         nc.scalar.dma_start(out=cat_sb[:, 0:32], in_=digits.rearrange("s b d -> (s b) d"))
@@ -263,27 +261,15 @@ def tile_decoder_w_kernel(
         def logs(q):
             x2 = x2s[q]
             for lo in range(0, GW, PIECE):
-                if q + 1 < NG:
-                    nc.scalar.activation(
-                        out=x2[:, :, lo : lo + PIECE], in_=x2[:, :, lo : lo + PIECE], func=ACT.Ln, bias=eps_t[:]
-                    )
-                else:
-                    nc.scalar.activation(
-                        out=x2[:, 0, lo : lo + PIECE], in_=x2[:, 0, lo : lo + PIECE], func=ACT.Ln, bias=eps_t[:]
-                    )
-                    for c in range(lo, lo + PIECE, 64):
-                        nc.scalar.activation(
-                            out=x2[:, 1, c : c + 64],
-                            in_=x2[:, 1, c : c + 64],
-                            func=ACT.Ln,
-                            bias=eps_t[:],
-                            accum_out=sum_l2[:, c // 64 : c // 64 + 1],
-                        )
+                nc.scalar.activation(
+                    out=x2[:, :, lo : lo + PIECE], in_=x2[:, :, lo : lo + PIECE], func=ACT.Ln, bias=eps_t[:]
+                )
 
         def difference(q, i):
             x2 = x2s[q]
             lo = PIECE * i
-            nc.gpsimd.tensor_tensor(
+            eng = nc.vector if 2 * PIECE * i < GW else nc.gpsimd
+            eng.tensor_tensor(
                 out=x2[:, 0, lo : lo + PIECE],
                 in0=x2[:, 0, lo : lo + PIECE],
                 in1=x2[:, 1, lo : lo + PIECE],
@@ -304,22 +290,13 @@ def tile_decoder_w_kernel(
             x2 = x2s[q]
             lo = PIECE * i
             j0 = (GW * q + lo) // 64
-            if q + 1 < NG:
-                nc.vector.tensor_reduce(
-                    out=loss[:, j0 : j0 + PIECE // 64],
-                    in_=x2[:, :, lo : lo + PIECE].rearrange("p a (j w) -> p j a w", w=64),
-                    axis=AX.XY,
-                    op=ALU.add,
-                    negate=True,
-                )
-            else:
-                nc.vector.tensor_reduce(
-                    out=sum_e[:, lo // 64 : (lo + PIECE) // 64],
-                    in_=x2[:, 0, lo : lo + PIECE].rearrange("p (j w) -> p j w", w=64),
-                    axis=AX.X,
-                    op=ALU.add,
-                    negate=True,
-                )
+            nc.vector.tensor_reduce(
+                out=loss[:, j0 : j0 + PIECE // 64],
+                in_=x2[:, :, lo : lo + PIECE].rearrange("p a (j w) -> p j a w", w=64),
+                axis=AX.XY,
+                op=ALU.add,
+                negate=True,
+            )
 
         vs = {}
         es = {}
@@ -342,13 +319,11 @@ def tile_decoder_w_kernel(
             es[b] = e
             rs[b] = a
 
-        def stage_b0(b):
+        def stage_b(b):
+            tb = work.tile([P, 512], BF16, name="tb")
             nc.vector.tensor_scalar(
                 out=es[b][:], in0=es[b][:], scalar1=1.0, scalar2=SA, op0=ALU.min, op1=ALU.mult
             )
-
-        def stage_b(b):
-            tb = work.tile([P, 512], BF16, name="tb")
             nc.vector.scalar_tensor_tensor(
                 out=tb[:], in0=es[b][:], scalar=-SA, in1=rs[b][:], op0=ALU.add, op1=ALU.add
             )
@@ -370,11 +345,9 @@ def tile_decoder_w_kernel(
             if i < 4:
                 stage_a(i)
             if 1 <= i < 5:
-                stage_b0(i - 1)
+                stage_b(i - 1)
             if 2 <= i < 6:
                 stage_c(i - 2)
-            if 1 <= i < 5:
-                stage_b(i - 1)
             if i >= 3:
                 l2_pass(0, i - 3)
 
@@ -401,6 +374,4 @@ def tile_decoder_w_kernel(
             if q + 1 < NG:
                 complements(q + 1)
             j0 = GW * q // 64
-            if q + 1 == NG:
-                nc.vector.tensor_tensor(out=loss[:, j0 : j0 + GW // 64], in0=sum_e[:], in1=sum_l2[:], op=ALU.subtract)
             nc.sync.dma_start(out=out_v[:, j0 : j0 + GW // 64], in_=loss[:, j0 : j0 + GW // 64])

@@ -47,9 +47,12 @@ def tile_decoder_w_kernel(
         w2pl = const.tile([P, 6144], U8, name="w2pl", align_bytes=64)
         rows = const.tile([P, 512], BF16, name="rows")
         rows_h = const.tile([P, 512], BF16, name="rows_h")
+        rows_1 = const.tile([P, P], BF16, name="rows_1")
+        b1T = const.tile([P, 16], BF16, name="b1T")
         eps_t = const.tile([P, 1], F32, name="eps_t")
         warm = const.tile([P, 1], F32, name="warm")
         nc.vector.memset(rows_h[:], 0.0)
+        nc.vector.memset(rows_1[:], 0.0)
         nc.vector.memset(rows[:], 0.0)
         nc.vector.memset(w1pl[:].bitcast(I32), 0)
         nc.vector.memset(w2pl[:].bitcast(I32), 0)
@@ -73,7 +76,7 @@ def tile_decoder_w_kernel(
         nc.scalar.dma_start(out=rows_h[0:8, :], in_=b_h.rearrange("(r n) -> r n", n=512))
         nc.scalar.dma_start(out=cat_sb[:, 0:32], in_=digits.rearrange("s b d -> (s b) d"))
         nc.scalar.dma_start(out=cat_sb[:, 32:128], in_=styles.rearrange("s b d -> (s b) d"))
-        nc.scalar.dma_start(out=rows[12:16, :], in_=b1.rearrange("(r n) -> r n", n=512))
+        nc.scalar.dma_start(out=rows_1[0:16, :], in_=b1.rearrange("(r n) -> r n", n=128))
         nc.scalar.dma_start(out=rows[0:12, :], in_=b2.rearrange("(r n) -> r n", n=512))
         nc.scalar.activation(out=warm[:], in_=eps_t[:], func=ACT.Exp)
         nc.sync.dma_start(out=wh[:], in_=W_h)
@@ -145,14 +148,27 @@ def tile_decoder_w_kernel(
                 start=True,
                 stop=True,
             )
-            if r < 12:
-                dst = b2b[:, 512 * r : 512 * (r + 1)]
-            else:
-                dst = b1b[:, 512 * (r - 12) : 512 * (r - 11)]
+            dst = b2b[:, 512 * r : 512 * (r + 1)]
             if r % 2 == 0:
                 nc.vector.tensor_copy(out=dst, in_=pb[:])
             else:
                 nc.scalar.copy(out=dst, in_=pb[:])
+
+        psd = misc.tile([P, P], BF16, name="psd", tag="misc")
+        nc.tensor.transpose(out=psd[:], in_=rows_1[:], identity=ident[:])
+        nc.vector.tensor_copy(out=b1T[:], in_=psd[:, 0:16])
+
+        def spread_b1(i):
+            pb = misc.tile([P, 4, P], BF16, name="pb1", tag="misc")
+            for k in range(4):
+                column = b1T[:, 4 * i + k : 4 * i + k + 1].to_broadcast([P, P])
+                nc.tensor.transpose(out=pb[:, k, :], in_=column, identity=ident[:])
+            dst = b1b[:, 512 * i : 512 * (i + 1)]
+            src = pb[:].rearrange("p k n -> p (k n)")
+            if i % 2 == 0:
+                nc.vector.tensor_copy(out=dst, in_=src)
+            else:
+                nc.scalar.copy(out=dst, in_=src)
 
         def layer0(g):
             ps0 = misc.tile([P, 4, P], F32, name="ps0", tag="misc")
@@ -199,7 +215,10 @@ def tile_decoder_w_kernel(
         for g in range(6):
             layer0(g + 2)
             for r in spread_order[4 * g : 4 * g + 4]:
-                spread(r)
+                if r < 12:
+                    spread(r)
+                else:
+                    spread_b1(r - 12)
             for b in range(4):
                 l1_pass(g, b, wt[g][:, 512 * b : 512 * (b + 1)])
             load_next(12 + g)
@@ -210,10 +229,7 @@ def tile_decoder_w_kernel(
         def l2_pass(q, g):
             for b in range(4):
                 if g == 0:
-                    if q % 2 == 0:
-                        ps_t = accp.tile([P, 512], F32, name="ps_a", tag="acc")
-                    else:
-                        ps_t = misc.tile([P, 512], F32, name="ps_m", tag="misc")
+                    ps_t = accp.tile([P, 512], F32, name="ps_a", tag="acc")
                     pss[(q, b)] = ps_t
                 col = GW * q + 512 * b
                 nc.tensor.matmul_mx(
@@ -268,7 +284,7 @@ def tile_decoder_w_kernel(
         def difference(q, i):
             x2 = x2s[q]
             lo = PIECE * i
-            eng = nc.vector if 2 * PIECE * i < GW else nc.gpsimd
+            eng = nc.gpsimd
             eng.tensor_tensor(
                 out=x2[:, 0, lo : lo + PIECE],
                 in0=x2[:, 0, lo : lo + PIECE],
@@ -276,13 +292,23 @@ def tile_decoder_w_kernel(
                 op=ALU.subtract,
             )
 
+        its = {}
+
+        def images_to_psum(q):
+            for c in range(2):
+                it = misc.tile([P, 2, 512], BF16, name="it", tag="misc")
+                for k in range(2):
+                    lo = GW * q + 1024 * c + 512 * k
+                    nc.tensor.matmul(out=it[:, k, :], lhsT=ident[:], rhs=img[:, lo : lo + 512], start=True, stop=True)
+                    its[(q, 2 * c + k)] = it[:, k, :]
+
         def weigh(q, i):
             x2 = x2s[q]
             lo = PIECE * i
             nc.vector.tensor_tensor(
                 out=x2[:, 0, lo : lo + PIECE],
                 in0=x2[:, 0, lo : lo + PIECE],
-                in1=img[:, GW * q + lo : GW * q + lo + PIECE],
+                in1=its[(q, i)],
                 op=ALU.mult,
             )
 
@@ -355,6 +381,7 @@ def tile_decoder_w_kernel(
         add_bias(0)
         sigmoids(0)
         complements(0)
+        images_to_psum(0)
         for q in range(NG):
             logs(q)
             if q + 1 < NG:
@@ -373,5 +400,6 @@ def tile_decoder_w_kernel(
                     total(q, k - 2)
             if q + 1 < NG:
                 complements(q + 1)
+                images_to_psum(q + 1)
             j0 = GW * q // 64
             nc.sync.dma_start(out=out_v[:, j0 : j0 + GW // 64], in_=loss[:, j0 : j0 + GW // 64])

@@ -1,3 +1,4 @@
+import math
 from contextlib import ExitStack
 
 import concourse.mybir as mybir
@@ -21,11 +22,12 @@ SELU_ALPHA = 1.6732632423543772848170429916717
 SELU_SCALE = 1.0507009873554804934193349852946
 SA = SELU_SCALE * SELU_ALPHA
 
+LN_SA = math.log(SA)
 PINNED = True
 GW = 2048
 NG = 3
 PIECE = 512
-SPLIT = 3
+SPLIT = 2
 Y_ON_VECTOR = False
 
 
@@ -64,7 +66,7 @@ def tile_decoder_w_kernel(
         catT = const.tile([P, P], BF16, name="catT")
         wh = const.tile([P, 4096], BF16, name="wh")
         bhT = const.tile([P, 4, 8], F32, name="bhT")
-        b1b = const.tile([P, 2048], BF16, name="b1b")
+        b1s = const.tile([P, 2048], F32, name="b1s")
         b2b = const.tile([P, 6144], BF16, name="b2b")
         img = const.tile([P, 6144], BF16, name="img")
         hcodes = const.tile([P, 8, P], U32, name="hcodes", align_bytes=64)
@@ -72,6 +74,8 @@ def tile_decoder_w_kernel(
         tcodes = const.tile([P, 4, P], U32, name="tcodes", align_bytes=64)
         tplanes = const.tile([P, 4, P], U8, name="tplanes", align_bytes=64)
         loss = const.tile([P, 96], F32, name="loss")
+        sum_b = const.tile([P, 32], F32, name="sum_b")
+        junk = const.tile([P, 64], F32, name="junk")
 
         nc.scalar.dma_start(out=rows_h[0:8, :], in_=b_h.rearrange("(r n) -> r n", n=512))
         nc.scalar.dma_start(out=cat_sb[:, 0:32], in_=digits.rearrange("s b d -> (s b) d"))
@@ -120,10 +124,14 @@ def tile_decoder_w_kernel(
                 q = k // 4
                 g = k % 4
                 t_ = wpool.tile([P, GW], U32, name="w2_%d" % k, tag="w", align_bytes=64)
-                nc.sync.dma_start(
-                    out=t_[:].bitcast(I32),
-                    in_=W2_words[g, :, GW * q : GW * (q + 1), :].rearrange("p n t -> p (n t)").bitcast(I32),
-                )
+                n_parts = 2 if k == 11 else 1
+                w = GW // n_parts
+                for h in range(n_parts):
+                    lo = GW * q + w * h
+                    nc.sync.dma_start(
+                        out=t_[:, w * h : w * (h + 1)].bitcast(I32),
+                        in_=W2_words[g, :, lo : lo + w, :].rearrange("p n t -> p (n t)").bitcast(I32),
+                    )
                 if g == 3:
                     nc.sync.dma_start(out=img[:, GW * q : GW * (q + 1)], in_=img_v[:, GW * q : GW * (q + 1)])
             wt[i] = t_
@@ -163,12 +171,12 @@ def tile_decoder_w_kernel(
             for k in range(4):
                 column = b1T[:, 4 * i + k : 4 * i + k + 1].to_broadcast([P, P])
                 nc.tensor.transpose(out=pb[:, k, :], in_=column, identity=ident[:])
-            dst = b1b[:, 512 * i : 512 * (i + 1)]
+            dst = b1s[:, 512 * i : 512 * (i + 1)]
             src = pb[:].rearrange("p k n -> p (k n)")
             if i % 2 == 0:
-                nc.vector.tensor_copy(out=dst, in_=src)
+                nc.vector.tensor_scalar(out=dst, in0=src, scalar1=SELU_SCALE, scalar2=None, op0=ALU.mult)
             else:
-                nc.scalar.copy(out=dst, in_=src)
+                nc.scalar.activation(out=dst, in_=src, func=ACT.Copy, scale=SELU_SCALE)
 
         def layer0(g):
             ps0 = misc.tile([P, 4, P], F32, name="ps0", tag="misc")
@@ -264,10 +272,10 @@ def tile_decoder_w_kernel(
         def complements(q):
             x2 = x2s[q]
             eng = nc.vector if Y_ON_VECTOR else nc.gpsimd
-            for lo in range(0, GW, 1024):
+            for lo in range(0, GW, 512):
                 eng.tensor_scalar(
-                    out=x2[:, 1, lo : lo + 1024],
-                    in0=x2[:, 0, lo : lo + 1024],
+                    out=x2[:, 1, lo : lo + 512],
+                    in0=x2[:, 0, lo : lo + 512],
                     scalar1=-1.0,
                     scalar2=1.0,
                     op0=ALU.mult,
@@ -284,7 +292,7 @@ def tile_decoder_w_kernel(
         def difference(q, i):
             x2 = x2s[q]
             lo = PIECE * i
-            eng = nc.gpsimd
+            eng = nc.vector if (q, i) == (2, 3) else nc.gpsimd
             eng.tensor_tensor(
                 out=x2[:, 0, lo : lo + PIECE],
                 in0=x2[:, 0, lo : lo + PIECE],
@@ -337,21 +345,27 @@ def tile_decoder_w_kernel(
         def stage_a(b):
             v = work.tile([P, 512], F32, name="v", bufs=3)
             e = work.tile([P, 512], F32, name="e", bufs=3)
-            a = work.tile([P, 512], F32, name="a", bufs=3)
-            nc.vector.tensor_tensor(out=v[:], in0=acc[b][:], in1=b1b[:, 512 * b : 512 * (b + 1)], op=ALU.add)
-            nc.scalar.activation(out=e[:], in_=v[:], func=ACT.Exp)
-            nc.scalar.activation(out=a[:], in_=v[:], func=ACT.Relu, scale=SELU_SCALE)
+            nc.vector.scalar_tensor_tensor(
+                out=v[:],
+                in0=acc[b][:],
+                scalar=SELU_SCALE,
+                in1=b1s[:, 512 * b : 512 * (b + 1)],
+                op0=ALU.mult,
+                op1=ALU.add,
+            )
+            nc.scalar.activation(out=e[:], in_=v[:], func=ACT.Exp, bias=LN_SA, scale=1.0 / SELU_SCALE)
             vs[b] = v
             es[b] = e
+
+        def stage_r(b):
+            a = work.tile([P, 512], F32, name="a", bufs=3)
+            nc.vector.tensor_scalar(out=a[:], in0=vs[b][:], scalar1=0.0, scalar2=-SA, op0=ALU.max, op1=ALU.add)
             rs[b] = a
 
         def stage_b(b):
             tb = work.tile([P, 512], BF16, name="tb")
-            nc.vector.tensor_scalar(
-                out=es[b][:], in0=es[b][:], scalar1=1.0, scalar2=SA, op0=ALU.min, op1=ALU.mult
-            )
             nc.vector.scalar_tensor_tensor(
-                out=tb[:], in0=es[b][:], scalar=-SA, in1=rs[b][:], op0=ALU.add, op1=ALU.add
+                out=tb[:], in0=es[b][:], scalar=SA, in1=rs[b][:], op0=ALU.min, op1=ALU.add
             )
             pst = misc.tile([P, 4, P], BF16, name="pst", tag="misc")
             for t in range(4):
@@ -372,10 +386,39 @@ def tile_decoder_w_kernel(
                 stage_a(i)
             if 1 <= i < 5:
                 stage_b(i - 1)
+            if i < 4:
+                stage_r(i)
+            if i == 4:
+                nc.scalar.activation(out=warm[:], in_=eps_t[:], func=ACT.Sigmoid)
             if 2 <= i < 6:
                 stage_c(i - 2)
             if i >= 3:
                 l2_pass(0, i - 3)
+
+        def total_d(i):
+            lo = PIECE * i
+            j = (4096 + lo) // 64
+            nc.vector.tensor_reduce(
+                out=loss[:, j : j + 8],
+                in_=x2s[2][:, 0, lo : lo + PIECE].rearrange("p (j w) -> p j w", w=64),
+                axis=AX.X,
+                op=ALU.add,
+                negate=True,
+            )
+
+        def total_b(i):
+            lo = PIECE * i
+            nc.vector.tensor_reduce(
+                out=sum_b[:, 8 * i : 8 * (i + 1)],
+                in_=x2s[2][:, 1, lo : lo + PIECE].rearrange("p (j w) -> p j w", w=64),
+                axis=AX.X,
+                op=ALU.add,
+            )
+
+        def total_b_on_scalar(i):
+            for j in range(8 * i, 8 * (i + 1)):
+                y = x2s[2][:, 1, 64 * j : 64 * (j + 1)]
+                nc.scalar.activation(out=junk[:], in_=y, func=ACT.Copy, accum_out=sum_b[:, j : j + 1])
 
         out_v = out.rearrange("s b c h -> (s b) (c h)")
         add_bias(0)
@@ -387,7 +430,27 @@ def tile_decoder_w_kernel(
             if q + 1 < NG:
                 for g in range(4):
                     l2_pass(q + 1, g)
+            j0 = GW * q // 64
             n_pieces = GW // PIECE
+            if q + 1 == NG:
+                total_b_on_scalar(2)
+                total_b_on_scalar(3)
+                for i in range(3):
+                    difference(q, i)
+                total_b(0)
+                weigh(q, 0)
+                total_b(1)
+                total_d(0)
+                weigh(q, 1)
+                weigh(q, 2)
+                total_d(1)
+                difference(q, 3)
+                total_d(2)
+                weigh(q, 3)
+                total_d(3)
+                nc.vector.tensor_tensor(out=loss[:, j0:96], in0=loss[:, j0:96], in1=sum_b[:], op=ALU.subtract)
+                nc.sync.dma_start(out=out_v[:, j0:96], in_=loss[:, j0:96])
+                continue
             for k in range(n_pieces + 2):
                 if k == SPLIT and q + 1 < NG:
                     add_bias(q + 1)
@@ -401,5 +464,4 @@ def tile_decoder_w_kernel(
             if q + 1 < NG:
                 complements(q + 1)
                 images_to_psum(q + 1)
-            j0 = GW * q // 64
             nc.sync.dma_start(out=out_v[:, j0 : j0 + GW // 64], in_=loss[:, j0 : j0 + GW // 64])

import math
from contextlib import ExitStack

import concourse.mybir as mybir
from concourse.masks import make_identity

FLOPS = 2 * 128 * (128 * 4096 + 4096 * 2048 + 2048 * 6144)

F32 = mybir.dt.float32
BF16 = mybir.dt.bfloat16
I32 = mybir.dt.int32
U32 = mybir.dt.uint32
U8 = mybir.dt.uint8
FP8X4 = mybir.dt.float8_e4m3fn_x4
ACT = mybir.ActivationFunctionType
ALU = mybir.AluOpType
AX = mybir.AxisListType

P = 128
EPS = 1e-9
SELU_ALPHA = 1.6732632423543772848170429916717
SELU_SCALE = 1.0507009873554804934193349852946
SA = SELU_SCALE * SELU_ALPHA

LN_SA = math.log(SA)
PINNED = True
GW = 2048
NG = 3
PIECE = 512
SPLIT = 2
Y_ON_VECTOR = False


def tile_decoder_w_kernel(
    tc, digits, styles, images, W_h, b_h, W1_words, W1_scales, b1, W2_words, W2_scales, b2, out
):
    nc = tc.nc
    with ExitStack() as ctx:
        if PINNED:
            ctx.enter_context(tc.manual_schedule())
        const = ctx.enter_context(tc.tile_pool(name="const", bufs=1))
        wpool = ctx.enter_context(tc.tile_pool(name="wpool", bufs=12))
        work = ctx.enter_context(tc.tile_pool(name="work", bufs=2))
        xpool = ctx.enter_context(tc.tile_pool(name="xpool", bufs=2))
        accp = ctx.enter_context(tc.psum_pool(name="accp", bufs=4))
        misc = ctx.enter_context(tc.psum_pool(name="misc", bufs=4))

        w1pl = const.tile([P, 2, 2048], U8, name="w1pl", align_bytes=64)
        w2pl = const.tile([P, 6144], U8, name="w2pl", align_bytes=64)
        rows = const.tile([P, 512], BF16, name="rows")
        rows_h = const.tile([P, 512], BF16, name="rows_h")
        rows_1 = const.tile([P, P], BF16, name="rows_1")
        b1T = const.tile([P, 16], BF16, name="b1T")
        eps_t = const.tile([P, 1], F32, name="eps_t")
        warm = const.tile([P, 1], F32, name="warm")
        nc.vector.memset(rows_h[:], 0.0)
        nc.vector.memset(rows_1[:], 0.0)
        nc.vector.memset(rows[:], 0.0)
        nc.vector.memset(w1pl[:].bitcast(I32), 0)
        nc.vector.memset(w2pl[:].bitcast(I32), 0)
        nc.vector.memset(eps_t[:], EPS)
        ident = const.tile([P, P], BF16, name="ident")
        make_identity(nc, ident[:])

        cat_sb = const.tile([P, P], BF16, name="cat_sb")
        catT = const.tile([P, P], BF16, name="catT")
        wh = const.tile([P, 4096], BF16, name="wh")
        bhT = const.tile([P, 4, 8], F32, name="bhT")
        b1s = const.tile([P, 2048], F32, name="b1s")
        b2b = const.tile([P, 6144], BF16, name="b2b")
        img = const.tile([P, 6144], BF16, name="img")
        hcodes = const.tile([P, 8, P], U32, name="hcodes", align_bytes=64)
        hplanes = const.tile([P, 8, P], U8, name="hplanes", align_bytes=64)
        tcodes = const.tile([P, 4, P], U32, name="tcodes", align_bytes=64)
        tplanes = const.tile([P, 4, P], U8, name="tplanes", align_bytes=64)
        loss = const.tile([P, 96], F32, name="loss")
        sum_b = const.tile([P, 32], F32, name="sum_b")
        junk = const.tile([P, 64], F32, name="junk")

        nc.scalar.dma_start(out=rows_h[0:8, :], in_=b_h.rearrange("(r n) -> r n", n=512))
        nc.scalar.dma_start(out=cat_sb[:, 0:32], in_=digits.rearrange("s b d -> (s b) d"))
        nc.scalar.dma_start(out=cat_sb[:, 32:128], in_=styles.rearrange("s b d -> (s b) d"))
        nc.scalar.dma_start(out=rows_1[0:16, :], in_=b1.rearrange("(r n) -> r n", n=128))
        nc.scalar.dma_start(out=rows[0:12, :], in_=b2.rearrange("(r n) -> r n", n=512))
        nc.scalar.activation(out=warm[:], in_=eps_t[:], func=ACT.Exp)
        nc.sync.dma_start(out=wh[:], in_=W_h)
        for q in range(4):
            nc.sync.dma_start(
                out=w1pl[32 * q : 32 * q + 16, 0, :].bitcast(I32),
                in_=W1_scales[0:4, 4 * q : 4 * q + 4, :].bitcast(I32),
            )
        for q in range(4):
            nc.gpsimd.dma_start(
                out=w1pl[32 * q : 32 * q + 16, 1, :].bitcast(F32),
                in_=W1_scales[4:8, 4 * q : 4 * q + 4, :].bitcast(F32),
            )
        for q in range(4):
            nc.gpsimd.dma_start(
                out=w2pl[32 * q : 32 * q + 16, :].bitcast(F32),
                in_=W2_scales[:, 4 * q : 4 * q + 4, :].bitcast(F32),
            )

        wt = {}
        img_v = images.rearrange("s b c h w -> (s b) (c h w)")

        def load_next(i):
            if i < 6:
                t_ = wpool.tile([P, 2048], U32, name="w1_%d" % i, tag="w", align_bytes=64)
                nc.sync.dma_start(
                    out=t_[:].bitcast(I32),
                    in_=W1_words[i].rearrange("p n t -> p (n t)").bitcast(I32),
                )
            elif i < 10:
                b = i - 6
                t_ = wpool.tile([P, 2, 512], U32, name="w1e_%d" % b, tag="w", align_bytes=64)
                nc.sync.dma_start(
                    out=t_[:].bitcast(I32),
                    in_=W1_words[6:8, :, 512 * b : 512 * (b + 1), :]
                    .rearrange("g p n t -> p g (n t)")
                    .bitcast(I32),
                )
            else:
                k = i - 10
                q = k // 4
                g = k % 4
                t_ = wpool.tile([P, GW], U32, name="w2_%d" % k, tag="w", align_bytes=64)
                n_parts = 2 if k == 11 else 1
                w = GW // n_parts
                for h in range(n_parts):
                    lo = GW * q + w * h
                    nc.sync.dma_start(
                        out=t_[:, w * h : w * (h + 1)].bitcast(I32),
                        in_=W2_words[g, :, lo : lo + w, :].rearrange("p n t -> p (n t)").bitcast(I32),
                    )
                if g == 3:
                    nc.sync.dma_start(out=img[:, GW * q : GW * (q + 1)], in_=img_v[:, GW * q : GW * (q + 1)])
            wt[i] = t_

        for i in range(12):
            load_next(i)

        psb = misc.tile([P, 4, P], BF16, name="psb", tag="misc")
        for t in range(4):
            nc.tensor.transpose(out=psb[:, t, :], in_=rows_h[:, t:512:4], identity=ident[:])
        nc.vector.tensor_copy(out=bhT[:], in_=psb[:, :, 0:8])
        psc = misc.tile([P, P], BF16, name="psc", tag="misc")
        nc.tensor.transpose(out=psc[:], in_=cat_sb[:], identity=ident[:])
        nc.vector.tensor_copy(out=catT[:], in_=psc[:])

        def spread(r):
            pb = misc.tile([P, 512], F32, name="pb", tag="misc")
            nc.tensor.matmul(
                out=pb[:],
                lhsT=ident[:, r : r + 1].to_broadcast([P, P]),
                rhs=rows[:],
                start=True,
                stop=True,
            )
            dst = b2b[:, 512 * r : 512 * (r + 1)]
            if r % 2 == 0:
                nc.vector.tensor_copy(out=dst, in_=pb[:])
            else:
                nc.scalar.copy(out=dst, in_=pb[:])

        psd = misc.tile([P, P], BF16, name="psd", tag="misc")
        nc.tensor.transpose(out=psd[:], in_=rows_1[:], identity=ident[:])
        nc.vector.tensor_copy(out=b1T[:], in_=psd[:, 0:16])

        def spread_b1(i):
            pb = misc.tile([P, 4, P], BF16, name="pb1", tag="misc")
            for k in range(4):
                column = b1T[:, 4 * i + k : 4 * i + k + 1].to_broadcast([P, P])
                nc.tensor.transpose(out=pb[:, k, :], in_=column, identity=ident[:])
            dst = b1s[:, 512 * i : 512 * (i + 1)]
            src = pb[:].rearrange("p k n -> p (k n)")
            if i % 2 == 0:
                nc.vector.tensor_scalar(out=dst, in0=src, scalar1=SELU_SCALE, scalar2=None, op0=ALU.mult)
            else:
                nc.scalar.activation(out=dst, in_=src, func=ACT.Copy, scale=SELU_SCALE)

        def layer0(g):
            ps0 = misc.tile([P, 4, P], F32, name="ps0", tag="misc")
            hb = work.tile([P, 4, P], BF16, name="hb")
            for t in range(4):
                nc.tensor.matmul(
                    out=ps0[:, t, :],
                    lhsT=wh[:, 512 * g + t : 512 * (g + 1) : 4],
                    rhs=catT[:],
                    start=True,
                    stop=True,
                )
            for t in range(4):
                nc.scalar.activation(
                    out=hb[:, t, :], in_=ps0[:, t, :], func=ACT.Relu, bias=bhT[:, t, g : g + 1]
                )
            hg = work.tile([P, P, 4], BF16, name="hg", align_bytes=64)
            nc.vector.tensor_copy(out=hg[:], in_=hb[:].rearrange("p t w -> p w t"))
            nc.vector.quantize_mx(
                out=hcodes[:, g, :].bitcast(FP8X4),
                scales=hplanes[:, g, :],
                in_=hg[:].rearrange("p w t -> p (w t)"),
            )

        acc = []
        for b in range(4):
            acc_t = accp.tile([P, 512], F32, name="acc%d" % b, tag="acc")
            acc.append(acc_t)

        def l1_pass(g, b, rhs):
            nc.tensor.matmul_mx(
                out=acc[b][:],
                lhsT=hcodes[:, g, :].bitcast(FP8X4),
                lhsT_scale=hplanes[:, g, :],
                rhs=rhs.bitcast(FP8X4),
                rhs_scale=w1pl[4 * (g % 4) : P, g // 4, 512 * b : 512 * (b + 1)],
                start=(g == 0),
                stop=(g == 7),
            )

        spread_order = [12, 13, 14, 15] + list(range(12))
        layer0(0)
        layer0(1)
        for g in range(6):
            layer0(g + 2)
            for r in spread_order[4 * g : 4 * g + 4]:
                if r < 12:
                    spread(r)
                else:
                    spread_b1(r - 12)
            for b in range(4):
                l1_pass(g, b, wt[g][:, 512 * b : 512 * (b + 1)])
            load_next(12 + g)

        x2s = {}
        pss = {}

        def l2_pass(q, g):
            for b in range(4):
                if g == 0:
                    ps_t = accp.tile([P, 512], F32, name="ps_a", tag="acc")
                    pss[(q, b)] = ps_t
                col = GW * q + 512 * b
                nc.tensor.matmul_mx(
                    out=pss[(q, b)][:],
                    lhsT=tcodes[:, g, :].bitcast(FP8X4),
                    lhsT_scale=tplanes[:, g, :],
                    rhs=wt[10 + 4 * q + g][:, 512 * b : 512 * (b + 1)].bitcast(FP8X4),
                    rhs_scale=w2pl[4 * g : P, col : col + 512],
                    start=(g == 0),
                    stop=(g == 3),
                )

        def add_bias(q):
            x2 = xpool.tile([P, 2, GW], F32, name="x2", tag="x2")
            x2s[q] = x2
            for b in range(4):
                col = GW * q + 512 * b
                nc.vector.tensor_tensor(
                    out=x2[:, 0, 512 * b : 512 * (b + 1)],
                    in0=pss[(q, b)][:],
                    in1=b2b[:, col : col + 512],
                    op=ALU.add,
                )

        def sigmoids(q):
            x2 = x2s[q]
            for lo in range(0, GW, 512):
                nc.scalar.activation(
                    out=x2[:, 0, lo : lo + 512], in_=x2[:, 0, lo : lo + 512], func=ACT.Sigmoid
                )

        def complements(q):
            x2 = x2s[q]
            eng = nc.vector if Y_ON_VECTOR else nc.gpsimd
            for lo in range(0, GW, 512):
                eng.tensor_scalar(
                    out=x2[:, 1, lo : lo + 512],
                    in0=x2[:, 0, lo : lo + 512],
                    scalar1=-1.0,
                    scalar2=1.0,
                    op0=ALU.mult,
                    op1=ALU.add,
                )

        def logs(q):
            x2 = x2s[q]
            for lo in range(0, GW, PIECE):
                nc.scalar.activation(
                    out=x2[:, :, lo : lo + PIECE], in_=x2[:, :, lo : lo + PIECE], func=ACT.Ln, bias=eps_t[:]
                )

        def difference(q, i):
            x2 = x2s[q]
            lo = PIECE * i
            eng = nc.vector if (q, i) == (2, 3) else nc.gpsimd
            eng.tensor_tensor(
                out=x2[:, 0, lo : lo + PIECE],
                in0=x2[:, 0, lo : lo + PIECE],
                in1=x2[:, 1, lo : lo + PIECE],
                op=ALU.subtract,
            )

        its = {}

        def images_to_psum(q):
            for c in range(2):
                it = misc.tile([P, 2, 512], BF16, name="it", tag="misc")
                for k in range(2):
                    lo = GW * q + 1024 * c + 512 * k
                    nc.tensor.matmul(out=it[:, k, :], lhsT=ident[:], rhs=img[:, lo : lo + 512], start=True, stop=True)
                    its[(q, 2 * c + k)] = it[:, k, :]

        def weigh(q, i):
            x2 = x2s[q]
            lo = PIECE * i
            nc.vector.tensor_tensor(
                out=x2[:, 0, lo : lo + PIECE],
                in0=x2[:, 0, lo : lo + PIECE],
                in1=its[(q, i)],
                op=ALU.mult,
            )

        def total(q, i):
            x2 = x2s[q]
            lo = PIECE * i
            j0 = (GW * q + lo) // 64
            nc.vector.tensor_reduce(
                out=loss[:, j0 : j0 + PIECE // 64],
                in_=x2[:, :, lo : lo + PIECE].rearrange("p a (j w) -> p j a w", w=64),
                axis=AX.XY,
                op=ALU.add,
                negate=True,
            )

        vs = {}
        es = {}
        rs = {}
        tgs = {}

        for b in range(4):
            for g in range(6, 8):
                l1_pass(g, b, wt[6 + b][:, g - 6, :])
            load_next(18 + b)

        def stage_a(b):
            v = work.tile([P, 512], F32, name="v", bufs=3)
            e = work.tile([P, 512], F32, name="e", bufs=3)
            nc.vector.scalar_tensor_tensor(
                out=v[:],
                in0=acc[b][:],
                scalar=SELU_SCALE,
                in1=b1s[:, 512 * b : 512 * (b + 1)],
                op0=ALU.mult,
                op1=ALU.add,
            )
            nc.scalar.activation(out=e[:], in_=v[:], func=ACT.Exp, bias=LN_SA, scale=1.0 / SELU_SCALE)
            vs[b] = v
            es[b] = e

        def stage_r(b):
            a = work.tile([P, 512], F32, name="a", bufs=3)
            nc.vector.tensor_scalar(out=a[:], in0=vs[b][:], scalar1=0.0, scalar2=-SA, op0=ALU.max, op1=ALU.add)
            rs[b] = a

        def stage_b(b):
            tb = work.tile([P, 512], BF16, name="tb")
            nc.vector.scalar_tensor_tensor(
                out=tb[:], in0=es[b][:], scalar=SA, in1=rs[b][:], op0=ALU.min, op1=ALU.add
            )
            pst = misc.tile([P, 4, P], BF16, name="pst", tag="misc")
            for t in range(4):
                nc.tensor.transpose(out=pst[:, t, :], in_=tb[:, t:512:4], identity=ident[:])
            tg = work.tile([P, P, 4], BF16, name="tg", align_bytes=64)
            nc.scalar.copy(out=tg[:], in_=pst[:].rearrange("p t w -> p w t"))
            tgs[b] = tg

        def stage_c(b):
            nc.vector.quantize_mx(
                out=tcodes[:, b, :].bitcast(FP8X4),
                scales=tplanes[:, b, :],
                in_=tgs[b][:].rearrange("p w t -> p (w t)"),
            )

        for i in range(7):
            if i < 4:
                stage_a(i)
            if 1 <= i < 5:
                stage_b(i - 1)
            if i < 4:
                stage_r(i)
            if i == 4:
                nc.scalar.activation(out=warm[:], in_=eps_t[:], func=ACT.Sigmoid)
            if 2 <= i < 6:
                stage_c(i - 2)
            if i >= 3:
                l2_pass(0, i - 3)

        def total_d(i):
            lo = PIECE * i
            j = (4096 + lo) // 64
            nc.vector.tensor_reduce(
                out=loss[:, j : j + 8],
                in_=x2s[2][:, 0, lo : lo + PIECE].rearrange("p (j w) -> p j w", w=64),
                axis=AX.X,
                op=ALU.add,
                negate=True,
            )

        def total_b(i):
            lo = PIECE * i
            nc.vector.tensor_reduce(
                out=sum_b[:, 8 * i : 8 * (i + 1)],
                in_=x2s[2][:, 1, lo : lo + PIECE].rearrange("p (j w) -> p j w", w=64),
                axis=AX.X,
                op=ALU.add,
            )

        def total_b_on_scalar(i):
            for j in range(8 * i, 8 * (i + 1)):
                y = x2s[2][:, 1, 64 * j : 64 * (j + 1)]
                nc.scalar.activation(out=junk[:], in_=y, func=ACT.Copy, accum_out=sum_b[:, j : j + 1])

        out_v = out.rearrange("s b c h -> (s b) (c h)")
        add_bias(0)
        sigmoids(0)
        complements(0)
        images_to_psum(0)
        for q in range(NG):
            logs(q)
            if q + 1 < NG:
                for g in range(4):
                    l2_pass(q + 1, g)
            j0 = GW * q // 64
            n_pieces = GW // PIECE
            if q + 1 == NG:
                total_b_on_scalar(2)
                total_b_on_scalar(3)
                for i in range(3):
                    difference(q, i)
                total_b(0)
                weigh(q, 0)
                total_b(1)
                total_d(0)
                weigh(q, 1)
                weigh(q, 2)
                total_d(1)
                difference(q, 3)
                total_d(2)
                weigh(q, 3)
                total_d(3)
                nc.vector.tensor_tensor(out=loss[:, j0:96], in0=loss[:, j0:96], in1=sum_b[:], op=ALU.subtract)
                nc.sync.dma_start(out=out_v[:, j0:96], in_=loss[:, j0:96])
                continue
            for k in range(n_pieces + 2):
                if k == SPLIT and q + 1 < NG:
                    add_bias(q + 1)
                    sigmoids(q + 1)
                if k < n_pieces:
                    difference(q, k)
                if 1 <= k <= n_pieces:
                    weigh(q, k - 1)
                if k >= 2:
                    total(q, k - 2)
            if q + 1 < NG:
                complements(q + 1)
                images_to_psum(q + 1)
            nc.sync.dma_start(out=out_v[:, j0 : j0 + GW // 64], in_=loss[:, j0 : j0 + GW // 64])
